import numpy as np
import ml_dtypes

BF16 = ml_dtypes.bfloat16


def bf(x):
    return np.asarray(x, np.float32).astype(BF16)


def f32(x):
    return np.asarray(x, np.float32)


def f64(x):
    return np.asarray(x).astype(np.float64)


def striped(idx):
    return np.tile(idx.reshape(-1, 16).T, (8, 1))


A, B, C, H, S, N = 4, 128, 512, 256, 512, 256


def setup_inputs():
    return {"base": f32(0.2 * np.random.standard_normal((C, S))), "h": bf(np.maximum(np.random.standard_normal((H, B)), 0.0)), "w2": bf(2.5 * np.random.standard_normal((A, H, N)) / np.sqrt(H)), "corr": f32(np.random.standard_normal((A, N))), "offs": striped(np.random.permutation(S)[:N])}


def reference(base, h, w2, corr, offs):
    idx = offs[:16].T.reshape(-1)
    x = np.einsum("kt,akn->atn", f64(h), f64(w2)) + f64(corr)[:, None, :]
    e = np.exp(x - x.max(axis=-1, keepdims=True))
    p = e / e.sum(axis=-1, keepdims=True)
    out = f64(base).copy()
    out[:, idx] = p.reshape(C, N)
    return out

@@ -1,0 +1,71 @@
+import concourse.mybir as mybir
+
+P = 128
+EXPERTS = 4
+HIDDEN = 256
+K_BLOCKS = HIDDEN // P
+LISTED = 256
+POLICIES = 512
+
+FLOPS = 2 * EXPERTS * P * HIDDEN * LISTED
+
+F32 = mybir.dt.float32
+BF16 = mybir.dt.bfloat16
+U16 = mybir.dt.uint16
+
+
+def tile_nembnet_kernel(tc, base, h, w2, corr, offs, out):
+    nc = tc.nc
+    with (
+        tc.tile_pool(name="held", bufs=1) as held,
+        tc.tile_pool(name="soft", bufs=EXPERTS) as soft,
+        tc.psum_pool(name="banks", bufs=EXPERTS) as banks,
+    ):
+        offsets = held.tile([P, LISTED // 16], U16, name="offsets")
+        nc.sync.dma_start(offsets[:], offs)
+        corr_row = held.tile([1, EXPERTS, LISTED], F32, name="corr_row")
+        nc.sync.dma_start(corr_row[:], corr.unsqueeze(0))
+        hidden = held.tile([P, K_BLOCKS, P], BF16, name="hidden")
+        nc.sync.dma_start(hidden[:], h.rearrange("(kb p) t -> p kb t", p=P))
+        heads = []
+        windows = []
+        for a in range(EXPERTS):
+            head = held.tile([P, K_BLOCKS, LISTED], BF16, name=f"head{a}")
+            nc.sync.dma_start(head[:], w2[a].rearrange("(kb p) j -> p kb j", p=P))
+            heads.append(head)
+            window = held.tile([P, POLICIES], F32, name=f"window{a}")
+            nc.scalar.dma_start(window[:], base[a * P : (a + 1) * P, :])
+            windows.append(window)
+
+        ones_row = held.tile([1, P], F32, name="ones_row")
+        nc.vector.memset(ones_row[:], 1.0)
+        ones_tile = held.tile([P, LISTED], F32, name="ones_tile")
+        nc.gpsimd.memset(ones_tile[:], 1.0)
+
+        for a in range(EXPERTS):
+            scores = banks.tile([P, LISTED], F32, name="scores")
+            nc.tensor.matmul(scores[:], ones_row[:], corr_row[:, a, :], start=True, stop=False)
+            for kb in range(K_BLOCKS):
+                nc.tensor.matmul(
+                    scores[:], hidden[:, kb, :], heads[a][:, kb, :], start=False, stop=(kb == K_BLOCKS - 1)
+                )
+
+            neg_max = soft.tile([P, 1], F32, name="neg_max")
+            nc.vector.reduce_max(neg_max[:], scores[:], axis=mybir.AxisListType.X, negate=True)
+            expo = soft.tile([P, LISTED], F32, name="expo")
+            total = soft.tile([P, 1], F32, name="total")
+            nc.scalar.activation(
+                expo[:], scores[:], mybir.ActivationFunctionType.Exp, bias=neg_max[:], scale=1.0, accum_out=total[:]
+            )
+            inverse = soft.tile([P, 1], F32, name="inverse")
+            nc.vector.reciprocal(inverse[:], total[:])
+            inverse_row = soft.tile([P, LISTED], F32, name="inverse_row")
+            nc.scalar.activation(inverse_row[:], ones_tile[:], mybir.ActivationFunctionType.Copy, scale=inverse[:])
+
+            nc.vector.tensor_tensor(
+                windows[a][:].indirect(offsets[:]),
+                expo[:],
+                inverse_row[:],
+                mybir.AluOpType.mult,
+            )
+            nc.sync.dma_start(out[a * P : (a + 1) * P, :], windows[a][:])

@@ -18,54 +18,53 @@ def tile_nembnet_kernel(tc, base, h, w2, corr, offs, out):
     nc = tc.nc
     with (
         tc.tile_pool(name="held", bufs=1) as held,
-        tc.tile_pool(name="soft", bufs=EXPERTS) as soft,
+        tc.tile_pool(name="soft", bufs=2) as soft,
         tc.psum_pool(name="banks", bufs=EXPERTS) as banks,
     ):
+        hidden = held.tile([P, K_BLOCKS, P], BF16, name="hidden")
+        nc.sync.dma_start(hidden[:], h.rearrange("(p kb) t -> p kb t", kb=K_BLOCKS))
+        corr_row = held.tile([1, EXPERTS, LISTED], F32, name="corr_row")
+        nc.scalar.dma_start(corr_row[:], corr.unsqueeze(0))
+        first_head = held.tile([P, 1, K_BLOCKS, LISTED], BF16, name="first_head")
+        nc.sync.dma_start(first_head[:], w2[0:1].rearrange("a (p kb) j -> p a kb j", kb=K_BLOCKS))
+        other_heads = held.tile([P, EXPERTS - 1, K_BLOCKS, LISTED], BF16, name="other_heads")
+        nc.sync.dma_start(other_heads[:], w2[1:EXPERTS].rearrange("a (p kb) j -> p a kb j", kb=K_BLOCKS))
+        heads = [(first_head, 0)] + [(other_heads, a - 1) for a in range(1, EXPERTS)]
         offsets = held.tile([P, LISTED // 16], U16, name="offsets")
         nc.sync.dma_start(offsets[:], offs)
-        corr_row = held.tile([1, EXPERTS, LISTED], F32, name="corr_row")
-        nc.sync.dma_start(corr_row[:], corr.unsqueeze(0))
-        hidden = held.tile([P, K_BLOCKS, P], BF16, name="hidden")
-        nc.sync.dma_start(hidden[:], h.rearrange("(kb p) t -> p kb t", p=P))
-        heads = []
         windows = []
         for a in range(EXPERTS):
-            head = held.tile([P, K_BLOCKS, LISTED], BF16, name=f"head{a}")
-            nc.sync.dma_start(head[:], w2[a].rearrange("(kb p) j -> p kb j", p=P))
-            heads.append(head)
             window = held.tile([P, POLICIES], F32, name=f"window{a}")
-            nc.scalar.dma_start(window[:], base[a * P : (a + 1) * P, :])
+            queue = nc.scalar if a < EXPERTS - 1 else nc.sync
+            queue.dma_start(window[:], base[a * P : (a + 1) * P, :])
             windows.append(window)
 
         ones_row = held.tile([1, P], F32, name="ones_row")
         nc.vector.memset(ones_row[:], 1.0)
         ones_tile = held.tile([P, LISTED], F32, name="ones_tile")
-        nc.gpsimd.memset(ones_tile[:], 1.0)
+        nc.vector.memset(ones_tile[:], 1.0)
 
         for a in range(EXPERTS):
             scores = banks.tile([P, LISTED], F32, name="scores")
             nc.tensor.matmul(scores[:], ones_row[:], corr_row[:, a, :], start=True, stop=False)
+            head, place = heads[a]
             for kb in range(K_BLOCKS):
                 nc.tensor.matmul(
-                    scores[:], hidden[:, kb, :], heads[a][:, kb, :], start=False, stop=(kb == K_BLOCKS - 1)
+                    scores[:], hidden[:, kb, :], head[:, place, kb, :], start=False, stop=(kb == K_BLOCKS - 1)
                 )
 
-            neg_max = soft.tile([P, 1], F32, name="neg_max")
-            nc.vector.reduce_max(neg_max[:], scores[:], axis=mybir.AxisListType.X, negate=True)
-            expo = soft.tile([P, LISTED], F32, name="expo")
-            total = soft.tile([P, 1], F32, name="total")
+            work = soft.tile([P, 2 * LISTED + 3 * 8], F32, name="work")
+            expo = work[:, 0:LISTED]
+            inverse_row = work[:, LISTED : 2 * LISTED]
+            neg_max = work[:, 2 * LISTED : 2 * LISTED + 1]
+            total = work[:, 2 * LISTED + 8 : 2 * LISTED + 9]
+            inverse = work[:, 2 * LISTED + 16 : 2 * LISTED + 17]
+            nc.vector.reduce_max(neg_max, scores[:], axis=mybir.AxisListType.X, negate=True)
             nc.scalar.activation(
-                expo[:], scores[:], mybir.ActivationFunctionType.Exp, bias=neg_max[:], scale=1.0, accum_out=total[:]
+                expo, scores[:], mybir.ActivationFunctionType.Exp, bias=neg_max, scale=1.0, accum_out=total
             )
-            inverse = soft.tile([P, 1], F32, name="inverse")
-            nc.vector.reciprocal(inverse[:], total[:])
-            inverse_row = soft.tile([P, LISTED], F32, name="inverse_row")
-            nc.scalar.activation(inverse_row[:], ones_tile[:], mybir.ActivationFunctionType.Copy, scale=inverse[:])
+            nc.vector.reciprocal(inverse, total)
+            nc.vector.tensor_scalar_mul(inverse_row, ones_tile[:], inverse)
 
-            nc.vector.tensor_tensor(
-                windows[a][:].indirect(offsets[:]),
-                expo[:],
-                inverse_row[:],
-                mybir.AluOpType.mult,
-            )
+            nc.vector.tensor_tensor(windows[a][:].indirect(offsets[:]), expo, inverse_row, mybir.AluOpType.mult)
             nc.sync.dma_start(out[a * P : (a + 1) * P, :], windows[a][:])

@@ -23,13 +23,20 @@ def tile_nembnet_kernel(tc, base, h, w2, corr, offs, out):
     ):
         hidden = held.tile([P, K_BLOCKS, P], BF16, name="hidden")
         nc.sync.dma_start(hidden[:], h.rearrange("(p kb) t -> p kb t", kb=K_BLOCKS))
-        corr_row = held.tile([1, EXPERTS, LISTED], F32, name="corr_row")
-        nc.scalar.dma_start(corr_row[:], corr.unsqueeze(0))
-        first_head = held.tile([P, 1, K_BLOCKS, LISTED], BF16, name="first_head")
-        nc.sync.dma_start(first_head[:], w2[0:1].rearrange("a (p kb) j -> p a kb j", kb=K_BLOCKS))
-        other_heads = held.tile([P, EXPERTS - 1, K_BLOCKS, LISTED], BF16, name="other_heads")
-        nc.sync.dma_start(other_heads[:], w2[1:EXPERTS].rearrange("a (p kb) j -> p a kb j", kb=K_BLOCKS))
-        heads = [(first_head, 0)] + [(other_heads, a - 1) for a in range(1, EXPERTS)]
+
+        corr_rows = held.tile([P, EXPERTS * LISTED], F32, name="corr_rows")
+        nc.scalar.dma_start(corr_rows[0:32, :], corr.rearrange("a j -> (a j)").partition_broadcast(32))
+        nc.vector.memset(corr_rows[32:64, :], 0.0)
+        nc.gpsimd.memset(corr_rows[64:128, :], 0.0)
+        first_row = held.tile([P, P], F32, name="first_row")
+        nc.vector.memset(first_row[:], 0.0)
+        nc.vector.memset(first_row[0:1, :], 1.0)
+
+        heads = []
+        for a in range(EXPERTS):
+            head = held.tile([P, K_BLOCKS, LISTED], BF16, name=f"head{a}")
+            nc.sync.dma_start(head[:], w2[a].rearrange("(p kb) j -> p kb j", kb=K_BLOCKS))
+            heads.append(head)
         offsets = held.tile([P, LISTED // 16], U16, name="offsets")
         nc.sync.dma_start(offsets[:], offs)
         windows = []
@@ -39,18 +46,17 @@ def tile_nembnet_kernel(tc, base, h, w2, corr, offs, out):
             queue.dma_start(window[:], base[a * P : (a + 1) * P, :])
             windows.append(window)
 
-        ones_row = held.tile([1, P], F32, name="ones_row")
-        nc.vector.memset(ones_row[:], 1.0)
         ones_tile = held.tile([P, LISTED], F32, name="ones_tile")
-        nc.vector.memset(ones_tile[:], 1.0)
+        nc.gpsimd.memset(ones_tile[:], 1.0)
 
         for a in range(EXPERTS):
             scores = banks.tile([P, LISTED], F32, name="scores")
-            nc.tensor.matmul(scores[:], ones_row[:], corr_row[:, a, :], start=True, stop=False)
-            head, place = heads[a]
+            nc.tensor.matmul(
+                scores[:], first_row[:], corr_rows[:, a * LISTED : (a + 1) * LISTED], start=True, stop=False
+            )
             for kb in range(K_BLOCKS):
                 nc.tensor.matmul(
-                    scores[:], hidden[:, kb, :], head[:, place, kb, :], start=False, stop=(kb == K_BLOCKS - 1)
+                    scores[:], hidden[:, kb, :], heads[a][:, kb, :], start=False, stop=(kb == K_BLOCKS - 1)
                 )
 
             work = soft.tile([P, 2 * LISTED + 3 * 8], F32, name="work")

@@ -18,7 +18,7 @@ def tile_nembnet_kernel(tc, base, h, w2, corr, offs, out):
     nc = tc.nc
     with (
         tc.tile_pool(name="held", bufs=1) as held,
-        tc.tile_pool(name="soft", bufs=2) as soft,
+        tc.tile_pool(name="soft", bufs=EXPERTS) as soft,
         tc.psum_pool(name="banks", bufs=EXPERTS) as banks,
     ):
         hidden = held.tile([P, K_BLOCKS, P], BF16, name="hidden")
@@ -49,7 +49,9 @@ def tile_nembnet_kernel(tc, base, h, w2, corr, offs, out):
         ones_tile = held.tile([P, LISTED], F32, name="ones_tile")
         nc.gpsimd.memset(ones_tile[:], 1.0)
 
-        for a in range(EXPERTS):
+        works = []
+
+        def front(a):
             scores = banks.tile([P, LISTED], F32, name="scores")
             nc.tensor.matmul(
                 scores[:], first_row[:], corr_rows[:, a * LISTED : (a + 1) * LISTED], start=True, stop=False
@@ -58,19 +60,26 @@ def tile_nembnet_kernel(tc, base, h, w2, corr, offs, out):
                 nc.tensor.matmul(
                     scores[:], hidden[:, kb, :], heads[a][:, kb, :], start=False, stop=(kb == K_BLOCKS - 1)
                 )
-
             work = soft.tile([P, 2 * LISTED + 3 * 8], F32, name="work")
-            expo = work[:, 0:LISTED]
-            inverse_row = work[:, LISTED : 2 * LISTED]
+            works.append(work)
             neg_max = work[:, 2 * LISTED : 2 * LISTED + 1]
             total = work[:, 2 * LISTED + 8 : 2 * LISTED + 9]
-            inverse = work[:, 2 * LISTED + 16 : 2 * LISTED + 17]
             nc.vector.reduce_max(neg_max, scores[:], axis=mybir.AxisListType.X, negate=True)
             nc.scalar.activation(
-                expo, scores[:], mybir.ActivationFunctionType.Exp, bias=neg_max, scale=1.0, accum_out=total
+                work[:, 0:LISTED], scores[:], mybir.ActivationFunctionType.Exp, bias=neg_max, scale=1.0, accum_out=total
             )
+
+        front(0)
+        for a in range(EXPERTS):
+            work = works[a]
+            expo = work[:, 0:LISTED]
+            inverse_row = work[:, LISTED : 2 * LISTED]
+            total = work[:, 2 * LISTED + 8 : 2 * LISTED + 9]
+            inverse = work[:, 2 * LISTED + 16 : 2 * LISTED + 17]
             nc.vector.reciprocal(inverse, total)
             nc.vector.tensor_scalar_mul(inverse_row, ones_tile[:], inverse)
+            if a + 1 < EXPERTS:
+                front(a + 1)
 
             nc.vector.tensor_tensor(windows[a][:].indirect(offsets[:]), expo, inverse_row, mybir.AluOpType.mult)
             nc.sync.dma_start(out[a * P : (a + 1) * P, :], windows[a][:])

@@ -77,7 +77,7 @@ def tile_nembnet_kernel(tc, base, h, w2, corr, offs, out):
             total = work[:, 2 * LISTED + 8 : 2 * LISTED + 9]
             inverse = work[:, 2 * LISTED + 16 : 2 * LISTED + 17]
             nc.vector.reciprocal(inverse, total)
-            nc.vector.tensor_scalar_mul(inverse_row, ones_tile[:], inverse)
+            nc.scalar.activation(inverse_row, ones_tile[:], mybir.ActivationFunctionType.Copy, scale=inverse)
             if a + 1 < EXPERTS:
                 front(a + 1)
 

@@ -32,18 +32,18 @@ def tile_nembnet_kernel(tc, base, h, w2, corr, offs, out):
         nc.vector.memset(first_row[:], 0.0)
         nc.vector.memset(first_row[0:1, :], 1.0)
 
+        queues = [nc.sync, nc.scalar]
         heads = []
         for a in range(EXPERTS):
             head = held.tile([P, K_BLOCKS, LISTED], BF16, name=f"head{a}")
-            nc.sync.dma_start(head[:], w2[a].rearrange("(p kb) j -> p kb j", kb=K_BLOCKS))
+            queues[a % 2].dma_start(head[:], w2[a].rearrange("(p kb) j -> p kb j", kb=K_BLOCKS))
             heads.append(head)
         offsets = held.tile([P, LISTED // 16], U16, name="offsets")
         nc.sync.dma_start(offsets[:], offs)
         windows = []
         for a in range(EXPERTS):
             window = held.tile([P, POLICIES], F32, name=f"window{a}")
-            queue = nc.scalar if a < EXPERTS - 1 else nc.sync
-            queue.dma_start(window[:], base[a * P : (a + 1) * P, :])
+            queues[a % 2].dma_start(window[:], base[a * P : (a + 1) * P, :])
             windows.append(window)
 
         ones_tile = held.tile([P, LISTED], F32, name="ones_tile")

@@ -53,13 +53,11 @@ def tile_nembnet_kernel(tc, base, h, w2, corr, offs, out):
 
         def front(a):
             scores = banks.tile([P, LISTED], F32, name="scores")
-            nc.tensor.matmul(
-                scores[:], first_row[:], corr_rows[:, a * LISTED : (a + 1) * LISTED], start=True, stop=False
-            )
             for kb in range(K_BLOCKS):
-                nc.tensor.matmul(
-                    scores[:], hidden[:, kb, :], heads[a][:, kb, :], start=False, stop=(kb == K_BLOCKS - 1)
-                )
+                nc.tensor.matmul(scores[:], hidden[:, kb, :], heads[a][:, kb, :], start=(kb == 0), stop=False)
+            nc.tensor.matmul(
+                scores[:], first_row[:], corr_rows[:, a * LISTED : (a + 1) * LISTED], start=False, stop=True
+            )
             work = soft.tile([P, 2 * LISTED + 3 * 8], F32, name="work")
             works.append(work)
             neg_max = work[:, 2 * LISTED : 2 * LISTED + 1]

@@ -22,10 +22,9 @@ def tile_nembnet_kernel(tc, base, h, w2, corr, offs, out):
         tc.psum_pool(name="banks", bufs=EXPERTS) as banks,
     ):
         hidden = held.tile([P, K_BLOCKS, P], BF16, name="hidden")
-        nc.sync.dma_start(hidden[:], h.rearrange("(p kb) t -> p kb t", kb=K_BLOCKS))
+        nc.scalar.dma_start(hidden[:], h.rearrange("(p kb) t -> p kb t", kb=K_BLOCKS))
 
         corr_rows = held.tile([P, EXPERTS * LISTED], F32, name="corr_rows")
-        nc.scalar.dma_start(corr_rows[0:32, :], corr.rearrange("a j -> (a j)").partition_broadcast(32))
         nc.vector.memset(corr_rows[32:64, :], 0.0)
         nc.gpsimd.memset(corr_rows[64:128, :], 0.0)
         first_row = held.tile([P, P], F32, name="first_row")
@@ -38,6 +37,8 @@ def tile_nembnet_kernel(tc, base, h, w2, corr, offs, out):
             head = held.tile([P, K_BLOCKS, LISTED], BF16, name=f"head{a}")
             queues[a % 2].dma_start(head[:], w2[a].rearrange("(p kb) j -> p kb j", kb=K_BLOCKS))
             heads.append(head)
+            if a == 0:
+                nc.sync.dma_start(corr_rows[0:32, :], corr.rearrange("a j -> (a j)").partition_broadcast(32))
         offsets = held.tile([P, LISTED // 16], U16, name="offsets")
         nc.sync.dma_start(offsets[:], offs)
         windows = []

@@ -19,6 +19,7 @@ def tile_nembnet_kernel(tc, base, h, w2, corr, offs, out):
     with (
         tc.tile_pool(name="held", bufs=1) as held,
         tc.tile_pool(name="soft", bufs=EXPERTS) as soft,
+        tc.tile_pool(name="stats", bufs=2) as stats,
         tc.psum_pool(name="banks", bufs=EXPERTS) as banks,
     ):
         hidden = held.tile([P, K_BLOCKS, P], BF16, name="hidden")
@@ -51,6 +52,7 @@ def tile_nembnet_kernel(tc, base, h, w2, corr, offs, out):
         nc.gpsimd.memset(ones_tile[:], 1.0)
 
         works = []
+        totals = []
 
         def front(a):
             scores = banks.tile([P, LISTED], F32, name="scores")
@@ -59,10 +61,12 @@ def tile_nembnet_kernel(tc, base, h, w2, corr, offs, out):
             nc.tensor.matmul(
                 scores[:], first_row[:], corr_rows[:, a * LISTED : (a + 1) * LISTED], start=False, stop=True
             )
-            work = soft.tile([P, 2 * LISTED + 3 * 8], F32, name="work")
+            work = soft.tile([P, 2 * LISTED + 8], F32, name="work")
             works.append(work)
-            neg_max = work[:, 2 * LISTED : 2 * LISTED + 1]
-            total = work[:, 2 * LISTED + 8 : 2 * LISTED + 9]
+            stat = stats.tile([P, 2 * 8], F32, name="stat")
+            neg_max = stat[:, 0:1]
+            total = stat[:, 8:9]
+            totals.append(total)
             nc.vector.reduce_max(neg_max, scores[:], axis=mybir.AxisListType.X, negate=True)
             nc.scalar.activation(
                 work[:, 0:LISTED], scores[:], mybir.ActivationFunctionType.Exp, bias=neg_max, scale=1.0, accum_out=total
@@ -73,9 +77,8 @@ def tile_nembnet_kernel(tc, base, h, w2, corr, offs, out):
             work = works[a]
             expo = work[:, 0:LISTED]
             inverse_row = work[:, LISTED : 2 * LISTED]
-            total = work[:, 2 * LISTED + 8 : 2 * LISTED + 9]
-            inverse = work[:, 2 * LISTED + 16 : 2 * LISTED + 17]
-            nc.vector.reciprocal(inverse, total)
+            inverse = work[:, 2 * LISTED : 2 * LISTED + 1]
+            nc.vector.reciprocal(inverse, totals[a])
             nc.scalar.activation(inverse_row, ones_tile[:], mybir.ActivationFunctionType.Copy, scale=inverse)
             if a + 1 < EXPERTS:
                 front(a + 1)

@@ -13,6 +13,14 @@ F32 = mybir.dt.float32
 BF16 = mybir.dt.bfloat16
 U16 = mybir.dt.uint16
 
+LEVELS = 3
+GROUP = 32
+EARLY = 2
+
+
+def upper_halves(words):
+    return words.bitcast(BF16)[:, 1::2]
+
 
 def tile_nembnet_kernel(tc, base, h, w2, corr, offs, out):
     nc = tc.nc
@@ -25,12 +33,29 @@ def tile_nembnet_kernel(tc, base, h, w2, corr, offs, out):
         hidden = held.tile([P, K_BLOCKS, P], BF16, name="hidden")
         nc.scalar.dma_start(hidden[:], h.rearrange("(p kb) t -> p kb t", kb=K_BLOCKS))
 
-        corr_rows = held.tile([P, EXPERTS * LISTED], F32, name="corr_rows")
-        nc.vector.memset(corr_rows[32:64, :], 0.0)
-        nc.gpsimd.memset(corr_rows[64:128, :], 0.0)
-        first_row = held.tile([P, P], F32, name="first_row")
-        nc.vector.memset(first_row[:], 0.0)
-        nc.vector.memset(first_row[0:1, :], 1.0)
+        parts = held.tile([P, LISTED], F32, name="parts")
+
+        marks = held.tile([P, EXPERTS], F32, name="marks")
+        nc.gpsimd.memset(marks[:], 0.0)
+        for level in range(LEVELS):
+            nc.gpsimd.affine_select(
+                out=marks[:],
+                in_=marks[:],
+                pattern=[[-1, EXPERTS]],
+                compare_op=mybir.AluOpType.not_equal,
+                fill=1.0,
+                base=-GROUP * level,
+                channel_multiplier=1,
+            )
+        pick = held.tile([P, EXPERTS, P], BF16, name="pick")
+        nc.gpsimd.tensor_scalar(
+            out=pick[:],
+            in0=marks[:].unsqueeze(2).to_broadcast([P, EXPERTS, P]),
+            scalar1=1.0,
+            scalar2=0.0,
+            op0=mybir.AluOpType.mult,
+            op1=mybir.AluOpType.add,
+        )
 
         queues = [nc.sync, nc.scalar]
         heads = []
@@ -39,7 +64,7 @@ def tile_nembnet_kernel(tc, base, h, w2, corr, offs, out):
             queues[a % 2].dma_start(head[:], w2[a].rearrange("(p kb) j -> p kb j", kb=K_BLOCKS))
             heads.append(head)
             if a == 0:
-                nc.sync.dma_start(corr_rows[0:32, :], corr.rearrange("a j -> (a j)").partition_broadcast(32))
+                nc.sync.dma_start(parts[:], corr.unsqueeze(0).to_broadcast([P // EXPERTS, EXPERTS, LISTED]))
         offsets = held.tile([P, LISTED // 16], U16, name="offsets")
         nc.sync.dma_start(offsets[:], offs)
         windows = []
@@ -47,6 +72,10 @@ def tile_nembnet_kernel(tc, base, h, w2, corr, offs, out):
             window = held.tile([P, POLICIES], F32, name=f"window{a}")
             queues[a % 2].dma_start(window[:], base[a * P : (a + 1) * P, :])
             windows.append(window)
+
+        for level in range(1, LEVELS):
+            rows = parts[0 : P - GROUP * (level + 1), :]
+            nc.vector.tensor_tensor(rows, rows, upper_halves(rows), mybir.AluOpType.subtract)
 
         ones_tile = held.tile([P, LISTED], F32, name="ones_tile")
         nc.gpsimd.memset(ones_tile[:], 1.0)
@@ -56,11 +85,11 @@ def tile_nembnet_kernel(tc, base, h, w2, corr, offs, out):
 
         def front(a):
             scores = banks.tile([P, LISTED], F32, name="scores")
-            for kb in range(K_BLOCKS):
-                nc.tensor.matmul(scores[:], hidden[:, kb, :], heads[a][:, kb, :], start=(kb == 0), stop=False)
-            nc.tensor.matmul(
-                scores[:], first_row[:], corr_rows[:, a * LISTED : (a + 1) * LISTED], start=False, stop=True
-            )
+            products = [(hidden[:, kb, :], heads[a][:, kb, :]) for kb in range(K_BLOCKS)]
+            shift = [(pick[:, a, :], upper_halves(parts[:]))]
+            terms = products + shift if a < EARLY else shift + products
+            for i, (weights, moving) in enumerate(terms):
+                nc.tensor.matmul(scores[:], weights, moving, start=(i == 0), stop=(i == len(terms) - 1))
             work = soft.tile([P, 2 * LISTED + 8], F32, name="work")
             works.append(work)
             stat = stats.tile([P, 2 * 8], F32, name="stat")

@@ -35,7 +35,7 @@ def tile_nembnet_kernel(tc, base, h, w2, corr, offs, out):
 
         parts = held.tile([P, LISTED], F32, name="parts")
 
-        marks = held.tile([P, EXPERTS], F32, name="marks")
+        marks = held.tile([P, EXPERTS], BF16, name="marks")
         nc.gpsimd.memset(marks[:], 0.0)
         for level in range(LEVELS):
             nc.gpsimd.affine_select(
@@ -47,15 +47,6 @@ def tile_nembnet_kernel(tc, base, h, w2, corr, offs, out):
                 base=-GROUP * level,
                 channel_multiplier=1,
             )
-        pick = held.tile([P, EXPERTS, P], BF16, name="pick")
-        nc.gpsimd.tensor_scalar(
-            out=pick[:],
-            in0=marks[:].unsqueeze(2).to_broadcast([P, EXPERTS, P]),
-            scalar1=1.0,
-            scalar2=0.0,
-            op0=mybir.AluOpType.mult,
-            op1=mybir.AluOpType.add,
-        )
 
         queues = [nc.sync, nc.scalar]
         heads = []
@@ -86,7 +77,7 @@ def tile_nembnet_kernel(tc, base, h, w2, corr, offs, out):
         def front(a):
             scores = banks.tile([P, LISTED], F32, name="scores")
             products = [(hidden[:, kb, :], heads[a][:, kb, :]) for kb in range(K_BLOCKS)]
-            shift = [(pick[:, a, :], upper_halves(parts[:]))]
+            shift = [(marks[:, a : a + 1].to_broadcast([P, P]), upper_halves(parts[:]))]
             terms = products + shift if a < EARLY else shift + products
             for i, (weights, moving) in enumerate(terms):
                 nc.tensor.matmul(scores[:], weights, moving, start=(i == 0), stop=(i == len(terms) - 1))

@@ -14,7 +14,6 @@ BF16 = mybir.dt.bfloat16
 U16 = mybir.dt.uint16
 
 LEVELS = 3
-GROUP = 32
 EARLY = 2
 
 
@@ -34,6 +33,8 @@ def tile_nembnet_kernel(tc, base, h, w2, corr, offs, out):
         nc.scalar.dma_start(hidden[:], h.rearrange("(p kb) t -> p kb t", kb=K_BLOCKS))
 
         parts = held.tile([P, LISTED], F32, name="parts")
+        nc.vector.memset(parts[32:64, :], 0.0)
+        nc.vector.memset(parts[64:128, :], 0.0)
 
         marks = held.tile([P, EXPERTS], BF16, name="marks")
         nc.gpsimd.memset(marks[:], 0.0)
@@ -44,7 +45,7 @@ def tile_nembnet_kernel(tc, base, h, w2, corr, offs, out):
                 pattern=[[-1, EXPERTS]],
                 compare_op=mybir.AluOpType.not_equal,
                 fill=1.0,
-                base=-GROUP * level,
+                base=-EXPERTS * level,
                 channel_multiplier=1,
             )
 
@@ -55,7 +56,7 @@ def tile_nembnet_kernel(tc, base, h, w2, corr, offs, out):
             queues[a % 2].dma_start(head[:], w2[a].rearrange("(p kb) j -> p kb j", kb=K_BLOCKS))
             heads.append(head)
             if a == 0:
-                nc.sync.dma_start(parts[:], corr.unsqueeze(0).to_broadcast([P // EXPERTS, EXPERTS, LISTED]))
+                nc.sync.dma_start(parts[0:32, :], corr.unsqueeze(0).to_broadcast([32 // EXPERTS, EXPERTS, LISTED]))
         offsets = held.tile([P, LISTED // 16], U16, name="offsets")
         nc.sync.dma_start(offsets[:], offs)
         windows = []
@@ -65,7 +66,7 @@ def tile_nembnet_kernel(tc, base, h, w2, corr, offs, out):
             windows.append(window)
 
         for level in range(1, LEVELS):
-            rows = parts[0 : P - GROUP * (level + 1), :]
+            rows = parts[0 : EXPERTS * (LEVELS - level), :]
             nc.vector.tensor_tensor(rows, rows, upper_halves(rows), mybir.AluOpType.subtract)
 
         ones_tile = held.tile([P, LISTED], F32, name="ones_tile")

@@ -100,7 +100,17 @@ def tile_nembnet_kernel(tc, base, h, w2, corr, offs, out):
             inverse_row = work[:, LISTED : 2 * LISTED]
             inverse = work[:, 2 * LISTED : 2 * LISTED + 1]
             nc.vector.reciprocal(inverse, totals[a])
-            nc.scalar.activation(inverse_row, ones_tile[:], mybir.ActivationFunctionType.Copy, scale=inverse)
+            if a == 0:
+                nc.gpsimd.tensor_scalar(
+                    out=inverse_row,
+                    in0=ones_tile[:],
+                    scalar1=inverse,
+                    scalar2=0.0,
+                    op0=mybir.AluOpType.mult,
+                    op1=mybir.AluOpType.add,
+                )
+            else:
+                nc.scalar.activation(inverse_row, ones_tile[:], mybir.ActivationFunctionType.Copy, scale=inverse)
             if a + 1 < EXPERTS:
                 front(a + 1)
 

@@ -14,7 +14,10 @@ BF16 = mybir.dt.bfloat16
 U16 = mybir.dt.uint16
 
 LEVELS = 3
-EARLY = 2
+PIECES = 4
+WIDTH = LISTED // PIECES
+ROWS = EXPERTS * PIECES
+LEAD = 3
 
 
 def upper_halves(words):
@@ -32,20 +35,18 @@ def tile_nembnet_kernel(tc, base, h, w2, corr, offs, out):
         hidden = held.tile([P, K_BLOCKS, P], BF16, name="hidden")
         nc.scalar.dma_start(hidden[:], h.rearrange("(p kb) t -> p kb t", kb=K_BLOCKS))
 
-        parts = held.tile([P, LISTED], F32, name="parts")
-        nc.vector.memset(parts[32:64, :], 0.0)
-        nc.vector.memset(parts[64:128, :], 0.0)
+        parts = held.tile([P, WIDTH], F32, name="parts")
 
-        marks = held.tile([P, EXPERTS], BF16, name="marks")
+        marks = held.tile([P, ROWS], BF16, name="marks")
         nc.gpsimd.memset(marks[:], 0.0)
         for level in range(LEVELS):
             nc.gpsimd.affine_select(
                 out=marks[:],
                 in_=marks[:],
-                pattern=[[-1, EXPERTS]],
+                pattern=[[-1, ROWS]],
                 compare_op=mybir.AluOpType.not_equal,
                 fill=1.0,
-                base=-EXPERTS * level,
+                base=-ROWS * level,
                 channel_multiplier=1,
             )
 
@@ -56,7 +57,8 @@ def tile_nembnet_kernel(tc, base, h, w2, corr, offs, out):
             queues[a % 2].dma_start(head[:], w2[a].rearrange("(p kb) j -> p kb j", kb=K_BLOCKS))
             heads.append(head)
             if a == 0:
-                nc.sync.dma_start(parts[0:32, :], corr.unsqueeze(0).to_broadcast([32 // EXPERTS, EXPERTS, LISTED]))
+                short_rows = corr.rearrange("a (piece j) -> (a piece) j", piece=PIECES)
+                nc.sync.dma_start(parts[:], short_rows.unsqueeze(0).to_broadcast([P // ROWS, ROWS, WIDTH]))
         offsets = held.tile([P, LISTED // 16], U16, name="offsets")
         nc.sync.dma_start(offsets[:], offs)
         windows = []
@@ -66,7 +68,7 @@ def tile_nembnet_kernel(tc, base, h, w2, corr, offs, out):
             windows.append(window)
 
         for level in range(1, LEVELS):
-            rows = parts[0 : EXPERTS * (LEVELS - level), :]
+            rows = parts[0 : ROWS * (LEVELS - level), :]
             nc.vector.tensor_tensor(rows, rows, upper_halves(rows), mybir.AluOpType.subtract)
 
         ones_tile = held.tile([P, LISTED], F32, name="ones_tile")
@@ -77,11 +79,19 @@ def tile_nembnet_kernel(tc, base, h, w2, corr, offs, out):
 
         def front(a):
             scores = banks.tile([P, LISTED], F32, name="scores")
-            products = [(hidden[:, kb, :], heads[a][:, kb, :]) for kb in range(K_BLOCKS)]
-            shift = [(marks[:, a : a + 1].to_broadcast([P, P]), upper_halves(parts[:]))]
-            terms = products + shift if a < EARLY else shift + products
-            for i, (weights, moving) in enumerate(terms):
-                nc.tensor.matmul(scores[:], weights, moving, start=(i == 0), stop=(i == len(terms) - 1))
+            products = [(scores[:], hidden[:, kb, :], heads[a][:, kb, :]) for kb in range(K_BLOCKS)]
+            shift = [
+                (
+                    scores[:, piece * WIDTH : (piece + 1) * WIDTH],
+                    marks[:, a * PIECES + piece : a * PIECES + piece + 1].to_broadcast([P, P]),
+                    upper_halves(parts[:]),
+                )
+                for piece in range(PIECES)
+            ]
+            ahead = min(max(LEAD - a * K_BLOCKS, 0), K_BLOCKS)
+            terms = products[:ahead] + shift + products[ahead:]
+            for i, (columns, weights, moving) in enumerate(terms):
+                nc.tensor.matmul(columns, weights, moving, start=(i == 0), stop=(i == len(terms) - 1))
             work = soft.tile([P, 2 * LISTED + 8], F32, name="work")
             works.append(work)
             stat = stats.tile([P, 2 * 8], F32, name="stat")

import concourse.mybir as mybir

P = 128
EXPERTS = 4
HIDDEN = 256
K_BLOCKS = HIDDEN // P
LISTED = 256
POLICIES = 512

FLOPS = 2 * EXPERTS * P * HIDDEN * LISTED

F32 = mybir.dt.float32
BF16 = mybir.dt.bfloat16
U16 = mybir.dt.uint16

LEVELS = 3
PIECES = 4
WIDTH = LISTED // PIECES
ROWS = EXPERTS * PIECES
LEAD = 3


def upper_halves(words):
    return words.bitcast(BF16)[:, 1::2]


def tile_nembnet_kernel(tc, base, h, w2, corr, offs, out):
    nc = tc.nc
    with (
        tc.tile_pool(name="held", bufs=1) as held,
        tc.tile_pool(name="soft", bufs=EXPERTS) as soft,
        tc.tile_pool(name="stats", bufs=2) as stats,
        tc.psum_pool(name="banks", bufs=EXPERTS) as banks,
    ):
        hidden = held.tile([P, K_BLOCKS, P], BF16, name="hidden")
        nc.scalar.dma_start(hidden[:], h.rearrange("(p kb) t -> p kb t", kb=K_BLOCKS))

        parts = held.tile([P, WIDTH], F32, name="parts")

        marks = held.tile([P, ROWS], BF16, name="marks")
        nc.gpsimd.memset(marks[:], 0.0)
        for level in range(LEVELS):
            nc.gpsimd.affine_select(
                out=marks[:],
                in_=marks[:],
                pattern=[[-1, ROWS]],
                compare_op=mybir.AluOpType.not_equal,
                fill=1.0,
                base=-ROWS * level,
                channel_multiplier=1,
            )

        queues = [nc.sync, nc.scalar]
        heads = []
        for a in range(EXPERTS):
            head = held.tile([P, K_BLOCKS, LISTED], BF16, name=f"head{a}")
            queues[a % 2].dma_start(head[:], w2[a].rearrange("(p kb) j -> p kb j", kb=K_BLOCKS))
            heads.append(head)
            if a == 0:
                short_rows = corr.rearrange("a (piece j) -> (a piece) j", piece=PIECES)
                nc.sync.dma_start(parts[:], short_rows.unsqueeze(0).to_broadcast([P // ROWS, ROWS, WIDTH]))
        offsets = held.tile([P, LISTED // 16], U16, name="offsets")
        nc.sync.dma_start(offsets[:], offs)
        windows = []
        for a in range(EXPERTS):
            window = held.tile([P, POLICIES], F32, name=f"window{a}")
            queues[a % 2].dma_start(window[:], base[a * P : (a + 1) * P, :])
            windows.append(window)

        for level in range(1, LEVELS):
            rows = parts[0 : ROWS * (LEVELS - level), :]
            nc.vector.tensor_tensor(rows, rows, upper_halves(rows), mybir.AluOpType.subtract)

        ones_tile = held.tile([P, LISTED], F32, name="ones_tile")
        nc.gpsimd.memset(ones_tile[:], 1.0)

        works = []
        totals = []

        def front(a):
            scores = banks.tile([P, LISTED], F32, name="scores")
            products = [(scores[:], hidden[:, kb, :], heads[a][:, kb, :]) for kb in range(K_BLOCKS)]
            shift = [
                (
                    scores[:, piece * WIDTH : (piece + 1) * WIDTH],
                    marks[:, a * PIECES + piece : a * PIECES + piece + 1].to_broadcast([P, P]),
                    upper_halves(parts[:]),
                )
                for piece in range(PIECES)
            ]
            ahead = min(max(LEAD - a * K_BLOCKS, 0), K_BLOCKS)
            terms = products[:ahead] + shift + products[ahead:]
            for i, (columns, weights, moving) in enumerate(terms):
                nc.tensor.matmul(columns, weights, moving, start=(i == 0), stop=(i == len(terms) - 1))
            work = soft.tile([P, 2 * LISTED + 8], F32, name="work")
            works.append(work)
            stat = stats.tile([P, 2 * 8], F32, name="stat")
            neg_max = stat[:, 0:1]
            total = stat[:, 8:9]
            totals.append(total)
            nc.vector.reduce_max(neg_max, scores[:], axis=mybir.AxisListType.X, negate=True)
            nc.scalar.activation(
                work[:, 0:LISTED], scores[:], mybir.ActivationFunctionType.Exp, bias=neg_max, scale=1.0, accum_out=total
            )

        front(0)
        for a in range(EXPERTS):
            work = works[a]
            expo = work[:, 0:LISTED]
            inverse_row = work[:, LISTED : 2 * LISTED]
            inverse = work[:, 2 * LISTED : 2 * LISTED + 1]
            nc.vector.reciprocal(inverse, totals[a])
            if a == 0:
                nc.gpsimd.tensor_scalar(
                    out=inverse_row,
                    in0=ones_tile[:],
                    scalar1=inverse,
                    scalar2=0.0,
                    op0=mybir.AluOpType.mult,
                    op1=mybir.AluOpType.add,
                )
            else:
                nc.scalar.activation(inverse_row, ones_tile[:], mybir.ActivationFunctionType.Copy, scale=inverse)
            if a + 1 < EXPERTS:
                front(a + 1)

            nc.vector.tensor_tensor(windows[a][:].indirect(offsets[:]), expo, inverse_row, mybir.AluOpType.mult)
            nc.sync.dma_start(out[a * P : (a + 1) * P, :], windows[a][:])
